import numpy as np
import ml_dtypes

BF16 = ml_dtypes.bfloat16


def bf(x):
    return np.asarray(x, np.float32).astype(BF16)


def f32(x):
    return np.asarray(x, np.float32)


def f64(x):
    return np.asarray(x).astype(np.float64)


def striped(idx):
    return np.tile(idx.reshape(-1, 16).T, (8, 1))


D, C, NN, B, M, S, N = 256, 256, 512, 4, 4, 4096, 2048
P_EDGE = 0.03


def setup_inputs():
    x = bf(np.random.standard_normal((D, N)))
    adj = f32(np.random.random((NN, NN)) * (np.random.random((NN, NN)) < P_EDGE))
    w = bf(np.random.standard_normal((M, D, C)) * np.sqrt(2.0 / (D * M + C)))
    b = f32(0.1 * np.random.standard_normal((C, 1)))
    base = f32(np.random.standard_normal((C, S)))
    return {"x": x, "adj": adj, "w": w, "b": b, "base": base, "offs": striped(np.random.permutation(S)[:N])}


def reference(x, adj, w, b, base, offs):
    idx = offs[:16].T.reshape(-1)
    ah = f64(adj) + np.eye(NN)
    dis = 1.0 / np.sqrt(ah.sum(axis=1))
    sup = dis[:, None] * ah.T * dis[None, :]
    wf = f64(w)
    t0 = f64(x).reshape(D, B, NN)
    t1 = t0 @ sup.T
    t2 = 2.0 * (t1 @ sup.T) - t0
    t3 = 2.0 * (t2 @ sup.T) - t1
    own = wf[0].T @ t0.reshape(D, N) + f64(b)
    dif = wf[1].T @ t1.reshape(D, N) + wf[2].T @ t2.reshape(D, N) + wf[3].T @ t3.reshape(D, N)
    out = f64(base).copy()
    out[:, idx] = own + dif
    return out

@@ -1,0 +1,152 @@
+import concourse.mybir as mybir
+from concourse.masks import make_identity
+
+P = 128
+D, C = 256, 256
+NODES, B = 512, 4
+N = B * NODES
+S = 4096
+M = 4
+DB, CB, KB = D // P, C // P, NODES // P
+
+FLOPS = 2 * (3 * D * N * NODES + M * D * C * N)
+
+BF16, F32, U16 = mybir.dt.bfloat16, mybir.dt.float32, mybir.dt.uint16
+MULT, ADD, SUBTRACT = mybir.AluOpType.mult, mybir.AluOpType.add, mybir.AluOpType.subtract
+ACT = mybir.ActivationFunctionType
+
+
+def block(i):
+    return slice(i * P, (i + 1) * P)
+
+
+def sample(q):
+    return slice(q * NODES, (q + 1) * NODES)
+
+
+def tile_dgcn_b_kernel(tc, x, adj, w, b, base, offs, out):
+    nc = tc.nc
+    with (
+        tc.tile_pool(name="held", bufs=1) as held,
+        tc.psum_pool(name="stage_banks", bufs=3) as stage_banks,
+        tc.psum_pool(name="flip_banks", bufs=2) as flip_banks,
+        tc.psum_pool(name="proj_banks", bufs=3) as proj_banks,
+    ):
+        ah = [held.tile([P, NODES], F32, name=f"ah{kb}") for kb in range(KB)]
+        for kb in range(KB):
+            nc.sync.dma_start(ah[kb][:], adj[block(kb), :])
+
+        plain = [[held.tile([P, N], BF16, name=f"plain{m}_{db}") for db in range(DB)] for m in range(M)]
+        for q in range(B):
+            for db in range(DB):
+                nc.sync.dma_start(plain[0][db][:, sample(q)], x[block(db), sample(q)])
+
+        w_sb = held.tile([P, M, DB, C], BF16, name="w_sb")
+        nc.sync.dma_start(w_sb[:], w.rearrange("m (db p) c -> p m db c", p=P))
+
+        bias = [held.tile([P, 1], F32, name=f"bias{cb}") for cb in range(CB)]
+        for cb in range(CB):
+            nc.sync.dma_start(bias[cb][:], b[block(cb), :])
+
+        offsets = held.tile([P, N // 16], U16, name="offsets")
+        nc.sync.dma_start(offsets[:], offs)
+
+        window = [held.tile([P, S], F32, name=f"window{cb}") for cb in range(CB)]
+        for cb in range(CB):
+            nc.sync.dma_start(window[cb][:], base[block(cb), :])
+
+        ident_f32 = held.tile([P, P], F32, name="ident_f32")
+        make_identity(nc, ident_f32[:])
+        ident_bf16 = held.tile([P, P], BF16, name="ident_bf16")
+        make_identity(nc, ident_bf16[:])
+
+        row_sum = held.tile([P, KB], F32, name="row_sum")
+        for kb in range(KB):
+            nc.vector.reduce_sum(row_sum[:, kb : kb + 1], ah[kb][:], axis=mybir.AxisListType.X)
+        root = held.tile([P, KB], F32, name="root")
+        nc.scalar.activation(root[:], row_sum[:], ACT.Sqrt, bias=1.0)
+        dis = held.tile([P, KB], F32, name="dis")
+        nc.vector.reciprocal(dis[:], root[:])
+
+        for kb in range(KB):
+            nc.gpsimd.tensor_tensor(ah[kb][:, block(kb)], ah[kb][:, block(kb)], ident_f32[:], ADD)
+
+        dis_wide = held.tile([P, KB, P], F32, name="dis_wide")
+        nc.vector.tensor_copy(dis_wide[:], dis[:].unsqueeze(2).to_broadcast([P, KB, P]))
+        dis_row = stage_banks.tile([P, NODES], F32, name="dis_row", tag="stage")
+        for kb in range(KB):
+            nc.tensor.transpose(dis_row[:, block(kb)], dis_wide[:, kb, :], ident_f32[:])
+
+        sup_t = [held.tile([P, NODES], BF16, name=f"sup_t{kb}") for kb in range(KB)]
+        for kb in range(KB):
+            nc.vector.scalar_tensor_tensor(sup_t[kb][:], ah[kb][:], dis[:, kb : kb + 1], dis_row[:], MULT, MULT)
+
+        flipped = [[held.tile([P, KB, D], BF16, name=f"flipped{m}_{q}") for q in range(B)] for m in range(M - 1)]
+        t1_f32 = [held.tile([P, N], F32, name=f"t1_f32_{db}") for db in range(DB)]
+
+        def flip(m, q):
+            flip_bank = flip_banks.tile([P, KB, D], BF16, tag="flip")
+            for kb in range(KB):
+                for db in range(DB):
+                    nc.tensor.transpose(
+                        flip_bank[:, kb, block(db)], plain[m][db][:, block(q * KB + kb)], ident_bf16[:]
+                    )
+            nc.scalar.copy(flipped[m][q][:], flip_bank[:])
+
+        def diffuse(m, q):
+            for db in range(DB):
+                stage_bank = stage_banks.tile([P, NODES], F32, tag="stage")
+                for kb in range(KB):
+                    nc.tensor.matmul(
+                        stage_bank[:],
+                        flipped[m - 1][q][:, kb, block(db)],
+                        sup_t[kb][:],
+                        start=(kb == 0),
+                        stop=(kb == KB - 1),
+                    )
+                rounded = plain[m][db][:, sample(q)]
+                if m == 1:
+                    nc.vector.tensor_copy(rounded, stage_bank[:])
+                    nc.scalar.copy(t1_f32[db][:, sample(q)], stage_bank[:])
+                else:
+                    two_back = plain[0] if m == 2 else t1_f32
+                    nc.vector.scalar_tensor_tensor(
+                        rounded, stage_bank[:], 2.0, two_back[db][:, sample(q)], MULT, SUBTRACT
+                    )
+
+        for q in range(B):
+            flip(0, q)
+        turns = [(m, q) for m in range(1, M) for q in range(B)]
+        for i, (m, q) in enumerate(turns):
+            diffuse(m, q)
+            if i > 0 and turns[i - 1][0] < M - 1:
+                flip(*turns[i - 1])
+
+        for cb in range(CB):
+            own = held.tile([P, N], F32, name=f"own{cb}")
+            dif = held.tile([P, N], F32, name=f"dif{cb}")
+            for q in range(B):
+                own_bank = proj_banks.tile([P, NODES], F32, tag="proj")
+                for db in range(DB):
+                    nc.tensor.matmul(
+                        own_bank[:],
+                        w_sb[:, 0, db, block(cb)],
+                        plain[0][db][:, sample(q)],
+                        start=(db == 0),
+                        stop=(db == DB - 1),
+                    )
+                nc.scalar.activation(own[:, sample(q)], own_bank[:], ACT.Identity, bias=bias[cb][:])
+            terms = [(m, db) for m in range(1, M) for db in range(DB)]
+            for q in range(B):
+                dif_bank = proj_banks.tile([P, NODES], F32, tag="proj")
+                for i, (m, db) in enumerate(terms):
+                    nc.tensor.matmul(
+                        dif_bank[:],
+                        w_sb[:, m, db, block(cb)],
+                        plain[m][db][:, sample(q)],
+                        start=(i == 0),
+                        stop=(i == len(terms) - 1),
+                    )
+                nc.scalar.copy(dif[:, sample(q)], dif_bank[:])
+            nc.vector.tensor_tensor(window[cb][:].indirect(offsets[:]), own[:], dif[:], ADD)
+            nc.sync.dma_start(out[block(cb), :], window[cb][:])

@@ -37,16 +37,17 @@ def tile_dgcn_b_kernel(tc, x, adj, w, b, base, offs, out):
             nc.sync.dma_start(ah[kb][:], adj[block(kb), :])
 
         plain = [[held.tile([P, N], BF16, name=f"plain{m}_{db}") for db in range(DB)] for m in range(M)]
+        w_sb = held.tile([P, M, DB, C], BF16, name="w_sb")
+        w_view = w.rearrange("m (db p) c -> p m db c", p=P)
+        bias = [held.tile([P, 1], F32, name=f"bias{cb}") for cb in range(CB)]
         for q in range(B):
             for db in range(DB):
                 nc.sync.dma_start(plain[0][db][:, sample(q)], x[block(db), sample(q)])
-
-        w_sb = held.tile([P, M, DB, C], BF16, name="w_sb")
-        nc.sync.dma_start(w_sb[:], w.rearrange("m (db p) c -> p m db c", p=P))
-
-        bias = [held.tile([P, 1], F32, name=f"bias{cb}") for cb in range(CB)]
-        for cb in range(CB):
-            nc.sync.dma_start(bias[cb][:], b[block(cb), :])
+            if q == 0:
+                nc.sync.dma_start(w_sb[:, 0:1], w_view[:, 0:1])
+                for cb in range(CB):
+                    nc.sync.dma_start(bias[cb][:], b[block(cb), :])
+        nc.sync.dma_start(w_sb[:, 1:M], w_view[:, 1:M])
 
         offsets = held.tile([P, N // 16], U16, name="offsets")
         nc.sync.dma_start(offsets[:], offs)
@@ -55,34 +56,16 @@ def tile_dgcn_b_kernel(tc, x, adj, w, b, base, offs, out):
         for cb in range(CB):
             nc.sync.dma_start(window[cb][:], base[block(cb), :])
 
-        ident_f32 = held.tile([P, P], F32, name="ident_f32")
-        make_identity(nc, ident_f32[:])
         ident_bf16 = held.tile([P, P], BF16, name="ident_bf16")
         make_identity(nc, ident_bf16[:])
-
-        row_sum = held.tile([P, KB], F32, name="row_sum")
-        for kb in range(KB):
-            nc.vector.reduce_sum(row_sum[:, kb : kb + 1], ah[kb][:], axis=mybir.AxisListType.X)
-        root = held.tile([P, KB], F32, name="root")
-        nc.scalar.activation(root[:], row_sum[:], ACT.Sqrt, bias=1.0)
-        dis = held.tile([P, KB], F32, name="dis")
-        nc.vector.reciprocal(dis[:], root[:])
-
-        for kb in range(KB):
-            nc.gpsimd.tensor_tensor(ah[kb][:, block(kb)], ah[kb][:, block(kb)], ident_f32[:], ADD)
-
-        dis_wide = held.tile([P, KB, P], F32, name="dis_wide")
-        nc.vector.tensor_copy(dis_wide[:], dis[:].unsqueeze(2).to_broadcast([P, KB, P]))
-        dis_row = stage_banks.tile([P, NODES], F32, name="dis_row", tag="stage")
-        for kb in range(KB):
-            nc.tensor.transpose(dis_row[:, block(kb)], dis_wide[:, kb, :], ident_f32[:])
-
-        sup_t = [held.tile([P, NODES], BF16, name=f"sup_t{kb}") for kb in range(KB)]
-        for kb in range(KB):
-            nc.vector.scalar_tensor_tensor(sup_t[kb][:], ah[kb][:], dis[:, kb : kb + 1], dis_row[:], MULT, MULT)
+        ident_f32 = held.tile([P, P], F32, name="ident_f32")
+        make_identity(nc, ident_f32[:])
 
         flipped = [[held.tile([P, KB, D], BF16, name=f"flipped{m}_{q}") for q in range(B)] for m in range(M - 1)]
         t1_f32 = [held.tile([P, N], F32, name=f"t1_f32_{db}") for db in range(DB)]
+        sup_t = [held.tile([P, NODES], BF16, name=f"sup_t{kb}") for kb in range(KB)]
+        own = [held.tile([P, N], F32, name=f"own{cb}") for cb in range(CB)]
+        dif = [held.tile([P, N], F32, name=f"dif{cb}") for cb in range(CB)]
 
         def flip(m, q):
             flip_bank = flip_banks.tile([P, KB, D], BF16, tag="flip")
@@ -114,8 +97,52 @@ def tile_dgcn_b_kernel(tc, x, adj, w, b, base, offs, out):
                         rounded, stage_bank[:], 2.0, two_back[db][:, sample(q)], MULT, SUBTRACT
                     )
 
-        for q in range(B):
+        def project(cb, q, stages):
+            proj_bank = proj_banks.tile([P, NODES], F32, tag="proj")
+            terms = [(m, db) for m in stages for db in range(DB)]
+            for i, (m, db) in enumerate(terms):
+                nc.tensor.matmul(
+                    proj_bank[:],
+                    w_sb[:, m, db, block(cb)],
+                    plain[m][db][:, sample(q)],
+                    start=(i == 0),
+                    stop=(i == len(terms) - 1),
+                )
+            return proj_bank
+
+        def project_own(cb, q):
+            nc.scalar.activation(own[cb][:, sample(q)], project(cb, q, [0])[:], ACT.Identity, bias=bias[cb][:])
+
+        def project_dif(cb, q):
+            nc.scalar.copy(dif[cb][:, sample(q)], project(cb, q, [1, 2, 3])[:])
+
+
+        row_sum = held.tile([P, KB], F32, name="row_sum")
+        for kb in range(KB):
+            nc.vector.reduce_sum(row_sum[:, kb : kb + 1], ah[kb][:], axis=mybir.AxisListType.X)
+        root = held.tile([P, KB], F32, name="root")
+        nc.scalar.activation(root[:], row_sum[:], ACT.Sqrt, bias=1.0)
+        dis = held.tile([P, KB], F32, name="dis")
+        nc.vector.reciprocal(dis[:], root[:])
+
+        for kb in range(KB):
+            nc.gpsimd.tensor_tensor(ah[kb][:, block(kb)], ah[kb][:, block(kb)], ident_f32[:], ADD)
+
+        flip(0, 0)
+        project_own(0, 0)
+
+        dis_wide = held.tile([P, KB, P], F32, name="dis_wide")
+        nc.vector.tensor_copy(dis_wide[:], dis[:].unsqueeze(2).to_broadcast([P, KB, P]))
+        dis_row = stage_banks.tile([P, NODES], F32, name="dis_row", tag="stage")
+        for kb in range(KB):
+            nc.tensor.transpose(dis_row[:, block(kb)], dis_wide[:, kb, :], ident_f32[:])
+        for kb in range(KB):
+            nc.vector.scalar_tensor_tensor(sup_t[kb][:], ah[kb][:], dis[:, kb : kb + 1], dis_row[:], MULT, MULT)
+
+        for q in range(1, B):
             flip(0, q)
+            project_own(0, q)
+
         turns = [(m, q) for m in range(1, M) for q in range(B)]
         for i, (m, q) in enumerate(turns):
             diffuse(m, q)
@@ -123,30 +150,9 @@ def tile_dgcn_b_kernel(tc, x, adj, w, b, base, offs, out):
                 flip(*turns[i - 1])
 
         for cb in range(CB):
-            own = held.tile([P, N], F32, name=f"own{cb}")
-            dif = held.tile([P, N], F32, name=f"dif{cb}")
             for q in range(B):
-                own_bank = proj_banks.tile([P, NODES], F32, tag="proj")
-                for db in range(DB):
-                    nc.tensor.matmul(
-                        own_bank[:],
-                        w_sb[:, 0, db, block(cb)],
-                        plain[0][db][:, sample(q)],
-                        start=(db == 0),
-                        stop=(db == DB - 1),
-                    )
-                nc.scalar.activation(own[:, sample(q)], own_bank[:], ACT.Identity, bias=bias[cb][:])
-            terms = [(m, db) for m in range(1, M) for db in range(DB)]
-            for q in range(B):
-                dif_bank = proj_banks.tile([P, NODES], F32, tag="proj")
-                for i, (m, db) in enumerate(terms):
-                    nc.tensor.matmul(
-                        dif_bank[:],
-                        w_sb[:, m, db, block(cb)],
-                        plain[m][db][:, sample(q)],
-                        start=(i == 0),
-                        stop=(i == len(terms) - 1),
-                    )
-                nc.scalar.copy(dif[:, sample(q)], dif_bank[:])
-            nc.vector.tensor_tensor(window[cb][:].indirect(offsets[:]), own[:], dif[:], ADD)
+                if cb > 0:
+                    project_own(cb, q)
+                project_dif(cb, q)
+            nc.vector.tensor_tensor(window[cb][:].indirect(offsets[:]), own[cb][:], dif[cb][:], ADD)
             nc.sync.dma_start(out[block(cb), :], window[cb][:])

@@ -11,6 +11,8 @@ DB, CB, KB = D // P, C // P, NODES // P
 
 FLOPS = 2 * (3 * D * N * NODES + M * D * C * N)
 
+WARM_UP = 12
+
 BF16, F32, U16 = mybir.dt.bfloat16, mybir.dt.float32, mybir.dt.uint16
 MULT, ADD, SUBTRACT = mybir.AluOpType.mult, mybir.AluOpType.add, mybir.AluOpType.subtract
 ACT = mybir.ActivationFunctionType
@@ -60,6 +62,12 @@ def tile_dgcn_b_kernel(tc, x, adj, w, b, base, offs, out):
         make_identity(nc, ident_bf16[:])
         ident_f32 = held.tile([P, P], F32, name="ident_f32")
         make_identity(nc, ident_f32[:])
+
+        zeros = held.tile([P, NODES], BF16, name="zeros")
+        nc.vector.memset(zeros[:], 0.0)
+        unread_bank = stage_banks.tile([P, NODES], F32, name="unread_bank", tag="stage")
+        for turn in range(WARM_UP):
+            nc.tensor.matmul(unread_bank[:], zeros[:, block(0)], zeros[:], start=True, stop=True)
 
         flipped = [[held.tile([P, KB, D], BF16, name=f"flipped{m}_{q}") for q in range(B)] for m in range(M - 1)]
         t1_f32 = [held.tile([P, N], F32, name=f"t1_f32_{db}") for db in range(DB)]

@@ -11,7 +11,7 @@ DB, CB, KB = D // P, C // P, NODES // P
 
 FLOPS = 2 * (3 * D * N * NODES + M * D * C * N)
 
-WARM_UP = 12
+WARM_UP = 9
 
 BF16, F32, U16 = mybir.dt.bfloat16, mybir.dt.float32, mybir.dt.uint16
 MULT, ADD, SUBTRACT = mybir.AluOpType.mult, mybir.AluOpType.add, mybir.AluOpType.subtract

@@ -11,10 +11,8 @@ DB, CB, KB = D // P, C // P, NODES // P
 
 FLOPS = 2 * (3 * D * N * NODES + M * D * C * N)
 
-WARM_UP = 9
-
 BF16, F32, U16 = mybir.dt.bfloat16, mybir.dt.float32, mybir.dt.uint16
-MULT, ADD, SUBTRACT = mybir.AluOpType.mult, mybir.AluOpType.add, mybir.AluOpType.subtract
+MULT, ADD = mybir.AluOpType.mult, mybir.AluOpType.add
 ACT = mybir.ActivationFunctionType
 
 
@@ -30,26 +28,25 @@ def tile_dgcn_b_kernel(tc, x, adj, w, b, base, offs, out):
     nc = tc.nc
     with (
         tc.tile_pool(name="held", bufs=1) as held,
-        tc.psum_pool(name="stage_banks", bufs=3) as stage_banks,
-        tc.psum_pool(name="flip_banks", bufs=2) as flip_banks,
-        tc.psum_pool(name="proj_banks", bufs=3) as proj_banks,
+        tc.psum_pool(name="banks", bufs=8) as banks,
     ):
-        ah = [held.tile([P, NODES], F32, name=f"ah{kb}") for kb in range(KB)]
-        for kb in range(KB):
-            nc.sync.dma_start(ah[kb][:], adj[block(kb), :])
-
-        plain = [[held.tile([P, N], BF16, name=f"plain{m}_{db}") for db in range(DB)] for m in range(M)]
         w_sb = held.tile([P, M, DB, C], BF16, name="w_sb")
         w_view = w.rearrange("m (db p) c -> p m db c", p=P)
-        bias = [held.tile([P, 1], F32, name=f"bias{cb}") for cb in range(CB)]
+        nc.sync.dma_start(w_sb[:, M - 1 : M], w_view[:, M - 1 : M])
+
+        x_sb = [held.tile([P, N], BF16, name=f"x_sb{db}") for db in range(DB)]
         for q in range(B):
             for db in range(DB):
-                nc.sync.dma_start(plain[0][db][:, sample(q)], x[block(db), sample(q)])
-            if q == 0:
-                nc.sync.dma_start(w_sb[:, 0:1], w_view[:, 0:1])
-                for cb in range(CB):
-                    nc.sync.dma_start(bias[cb][:], b[block(cb), :])
-        nc.sync.dma_start(w_sb[:, 1:M], w_view[:, 1:M])
+                nc.sync.dma_start(x_sb[db][:, sample(q)], x[block(db), sample(q)])
+
+        ah = [held.tile([P, NODES], F32, name=f"ah{kb}") for kb in range(KB)]
+        for kb in range(KB):
+            nc.scalar.dma_start(ah[kb][:], adj[block(kb), :])
+
+        nc.sync.dma_start(w_sb[:, 0 : M - 1], w_view[:, 0 : M - 1])
+        bias = [held.tile([P, 1], F32, name=f"bias{cb}") for cb in range(CB)]
+        for cb in range(CB):
+            nc.sync.dma_start(bias[cb][:], b[block(cb), :])
 
         offsets = held.tile([P, N // 16], U16, name="offsets")
         nc.sync.dma_start(offsets[:], offs)
@@ -58,72 +55,63 @@ def tile_dgcn_b_kernel(tc, x, adj, w, b, base, offs, out):
         for cb in range(CB):
             nc.sync.dma_start(window[cb][:], base[block(cb), :])
 
-        ident_bf16 = held.tile([P, P], BF16, name="ident_bf16")
-        make_identity(nc, ident_bf16[:])
         ident_f32 = held.tile([P, P], F32, name="ident_f32")
         make_identity(nc, ident_f32[:])
+        minus_half_ident = held.tile([P, P], BF16, name="minus_half_ident")
+        nc.gpsimd.tensor_scalar(minus_half_ident[:], ident_f32[:], -0.5, None, MULT)
 
-        zeros = held.tile([P, NODES], BF16, name="zeros")
-        nc.vector.memset(zeros[:], 0.0)
-        unread_bank = stage_banks.tile([P, NODES], F32, name="unread_bank", tag="stage")
-        for turn in range(WARM_UP):
-            nc.tensor.matmul(unread_bank[:], zeros[:, block(0)], zeros[:], start=True, stop=True)
+        def flipped_tiles(name):
+            return [
+                [held.tile([P, B * P], BF16, name=f"{name}_{cb}_{kb}") for kb in range(KB)] for cb in range(CB)
+            ]
 
-        flipped = [[held.tile([P, KB, D], BF16, name=f"flipped{m}_{q}") for q in range(B)] for m in range(M - 1)]
-        t1_f32 = [held.tile([P, N], F32, name=f"t1_f32_{db}") for db in range(DB)]
+        twice_b3, twice_b2, b1 = flipped_tiles("twice_b3"), flipped_tiles("twice_b2"), flipped_tiles("b1")
         sup_t = [held.tile([P, NODES], BF16, name=f"sup_t{kb}") for kb in range(KB)]
         own = [held.tile([P, N], F32, name=f"own{cb}") for cb in range(CB)]
         dif = [held.tile([P, N], F32, name=f"dif{cb}") for cb in range(CB)]
 
-        def flip(m, q):
-            flip_bank = flip_banks.tile([P, KB, D], BF16, tag="flip")
+        def open_flipped(m, cb, closes):
+            group = [banks.tile([P, B * P], F32, name=f"flipped_bank{nb}", tag="bank") for nb in range(KB)]
+            for q in range(B):
+                for nb in range(KB):
+                    for db in range(DB):
+                        nc.tensor.matmul(
+                            group[nb][:, block(q)],
+                            x_sb[db][:, block(q * KB + nb)],
+                            w_sb[:, m, db, block(cb)],
+                            start=(q == 0 and db == 0),
+                            stop=(closes and q == B - 1 and db == DB - 1),
+                        )
+            return group
+
+        def add_diffused(bank, nb, source):
             for kb in range(KB):
-                for db in range(DB):
-                    nc.tensor.transpose(
-                        flip_bank[:, kb, block(db)], plain[m][db][:, block(q * KB + kb)], ident_bf16[:]
-                    )
-            nc.scalar.copy(flipped[m][q][:], flip_bank[:])
-
-        def diffuse(m, q):
-            for db in range(DB):
-                stage_bank = stage_banks.tile([P, NODES], F32, tag="stage")
-                for kb in range(KB):
-                    nc.tensor.matmul(
-                        stage_bank[:],
-                        flipped[m - 1][q][:, kb, block(db)],
-                        sup_t[kb][:],
-                        start=(kb == 0),
-                        stop=(kb == KB - 1),
-                    )
-                rounded = plain[m][db][:, sample(q)]
-                if m == 1:
-                    nc.vector.tensor_copy(rounded, stage_bank[:])
-                    nc.scalar.copy(t1_f32[db][:, sample(q)], stage_bank[:])
-                else:
-                    two_back = plain[0] if m == 2 else t1_f32
-                    nc.vector.scalar_tensor_tensor(
-                        rounded, stage_bank[:], 2.0, two_back[db][:, sample(q)], MULT, SUBTRACT
-                    )
-
-        def project(cb, q, stages):
-            proj_bank = proj_banks.tile([P, NODES], F32, tag="proj")
-            terms = [(m, db) for m in stages for db in range(DB)]
-            for i, (m, db) in enumerate(terms):
                 nc.tensor.matmul(
-                    proj_bank[:],
-                    w_sb[:, m, db, block(cb)],
-                    plain[m][db][:, sample(q)],
-                    start=(i == 0),
-                    stop=(i == len(terms) - 1),
+                    bank[:], sup_t[kb][:, block(nb)], source[kb][:], start=False, stop=(kb == KB - 1)
                 )
-            return proj_bank
 
-        def project_own(cb, q):
-            nc.scalar.activation(own[cb][:, sample(q)], project(cb, q, [0])[:], ACT.Identity, bias=bias[cb][:])
+        def start_recurrence(cb):
+            group = open_flipped(3, cb, closes=True)
+            for nb in range(KB):
+                if nb % 2 == 0:
+                    nc.scalar.activation(twice_b3[cb][nb][:], group[nb][:], ACT.Copy, scale=2.0)
+                else:
+                    nc.vector.tensor_scalar(twice_b3[cb][nb][:], group[nb][:], 2.0, None, MULT)
 
-        def project_dif(cb, q):
-            nc.scalar.copy(dif[cb][:, sample(q)], project(cb, q, [1, 2, 3])[:])
+        def project_own(cb):
+            for q in range(B):
+                own_bank = banks.tile([P, NODES], F32, name="own_bank", tag="bank")
+                for db in range(DB):
+                    nc.tensor.matmul(
+                        own_bank[:],
+                        w_sb[:, 0, db, block(cb)],
+                        x_sb[db][:, sample(q)],
+                        start=(db == 0),
+                        stop=(db == DB - 1),
+                    )
+                nc.scalar.activation(own[cb][:, sample(q)], own_bank[:], ACT.Identity, bias=bias[cb][:])
 
+        start_recurrence(0)
 
         row_sum = held.tile([P, KB], F32, name="row_sum")
         for kb in range(KB):
@@ -136,31 +124,50 @@ def tile_dgcn_b_kernel(tc, x, adj, w, b, base, offs, out):
         for kb in range(KB):
             nc.gpsimd.tensor_tensor(ah[kb][:, block(kb)], ah[kb][:, block(kb)], ident_f32[:], ADD)
 
-        flip(0, 0)
-        project_own(0, 0)
-
         dis_wide = held.tile([P, KB, P], F32, name="dis_wide")
         nc.vector.tensor_copy(dis_wide[:], dis[:].unsqueeze(2).to_broadcast([P, KB, P]))
-        dis_row = stage_banks.tile([P, NODES], F32, name="dis_row", tag="stage")
+
+        start_recurrence(1)
+        project_own(0)
+
+        dis_row = banks.tile([P, NODES], F32, name="dis_row", tag="bank")
         for kb in range(KB):
             nc.tensor.transpose(dis_row[:, block(kb)], dis_wide[:, kb, :], ident_f32[:])
         for kb in range(KB):
             nc.vector.scalar_tensor_tensor(sup_t[kb][:], ah[kb][:], dis[:, kb : kb + 1], dis_row[:], MULT, MULT)
 
-        for q in range(1, B):
-            flip(0, q)
-            project_own(0, q)
-
-        turns = [(m, q) for m in range(1, M) for q in range(B)]
-        for i, (m, q) in enumerate(turns):
-            diffuse(m, q)
-            if i > 0 and turns[i - 1][0] < M - 1:
-                flip(*turns[i - 1])
-
         for cb in range(CB):
+            if cb > 0:
+                project_own(cb)
+
+            group = open_flipped(2, cb, closes=False)
+            for nb in range(KB):
+                add_diffused(group[nb], nb, twice_b3[cb])
+                nc.scalar.activation(twice_b2[cb][nb][:], group[nb][:], ACT.Copy, scale=2.0)
+
+            group = open_flipped(1, cb, closes=False)
+            for nb in range(KB):
+                add_diffused(group[nb], nb, twice_b2[cb])
+                nc.vector.scalar_tensor_tensor(
+                    b1[cb][nb][:], twice_b3[cb][nb][:], -0.5, group[nb][:], MULT, ADD
+                )
+
+            dif_banks = [banks.tile([P, NODES], F32, name=f"dif_bank{q}", tag="bank") for q in range(B)]
             for q in range(B):
-                if cb > 0:
-                    project_own(cb, q)
-                project_dif(cb, q)
+                for kb in range(KB):
+                    nc.tensor.matmul(
+                        dif_banks[q][:, block(kb)],
+                        twice_b2[cb][kb][:, block(q)],
+                        minus_half_ident[:],
+                        start=(kb == 0),
+                        stop=False,
+                    )
+            for q in range(B):
+                for kb in range(KB):
+                    nc.tensor.matmul(
+                        dif_banks[q][:], b1[cb][kb][:, block(q)], sup_t[kb][:], start=False, stop=(kb == KB - 1)
+                    )
+                nc.scalar.copy(dif[cb][:, sample(q)], dif_banks[q][:])
+
             nc.vector.tensor_tensor(window[cb][:].indirect(offsets[:]), own[cb][:], dif[cb][:], ADD)
             nc.sync.dma_start(out[block(cb), :], window[cb][:])

@@ -57,8 +57,8 @@ def tile_dgcn_b_kernel(tc, x, adj, w, b, base, offs, out):
 
         ident_f32 = held.tile([P, P], F32, name="ident_f32")
         make_identity(nc, ident_f32[:])
-        minus_half_ident = held.tile([P, P], BF16, name="minus_half_ident")
-        nc.gpsimd.tensor_scalar(minus_half_ident[:], ident_f32[:], -0.5, None, MULT)
+        ident_bf16 = held.tile([P, P], BF16, name="ident_bf16")
+        make_identity(nc, ident_bf16[:])
 
         def flipped_tiles(name):
             return [
@@ -67,6 +67,7 @@ def tile_dgcn_b_kernel(tc, x, adj, w, b, base, offs, out):
 
         twice_b3, twice_b2, b1 = flipped_tiles("twice_b3"), flipped_tiles("twice_b2"), flipped_tiles("b1")
         sup_t = [held.tile([P, NODES], BF16, name=f"sup_t{kb}") for kb in range(KB)]
+        twice_b2_plain = [held.tile([P, N], BF16, name=f"twice_b2_plain{cb}") for cb in range(CB)]
         own = [held.tile([P, N], F32, name=f"own{cb}") for cb in range(CB)]
         dif = [held.tile([P, N], F32, name=f"dif{cb}") for cb in range(CB)]
 
@@ -152,22 +153,21 @@ def tile_dgcn_b_kernel(tc, x, adj, w, b, base, offs, out):
                     b1[cb][nb][:], twice_b3[cb][nb][:], -0.5, group[nb][:], MULT, ADD
                 )
 
-            dif_banks = [banks.tile([P, NODES], F32, name=f"dif_bank{q}", tag="bank") for q in range(B)]
             for q in range(B):
+                plain_bank = banks.tile([P, NODES], BF16, name="plain_bank", tag="bank")
+                for kb in range(KB):
+                    nc.tensor.transpose(plain_bank[:, block(kb)], twice_b2[cb][kb][:, block(q)], ident_bf16[:])
+                nc.scalar.copy(twice_b2_plain[cb][:, sample(q)], plain_bank[:])
+
+            for q in range(B):
+                dif_bank = banks.tile([P, NODES], F32, name="dif_bank", tag="bank")
                 for kb in range(KB):
                     nc.tensor.matmul(
-                        dif_banks[q][:, block(kb)],
-                        twice_b2[cb][kb][:, block(q)],
-                        minus_half_ident[:],
-                        start=(kb == 0),
-                        stop=False,
+                        dif_bank[:], b1[cb][kb][:, block(q)], sup_t[kb][:], start=(kb == 0), stop=(kb == KB - 1)
                     )
-            for q in range(B):
-                for kb in range(KB):
-                    nc.tensor.matmul(
-                        dif_banks[q][:], b1[cb][kb][:, block(q)], sup_t[kb][:], start=False, stop=(kb == KB - 1)
-                    )
-                nc.scalar.copy(dif[cb][:, sample(q)], dif_banks[q][:])
+                nc.vector.scalar_tensor_tensor(
+                    dif[cb][:, sample(q)], twice_b2_plain[cb][:, sample(q)], -0.5, dif_bank[:], MULT, ADD
+                )
 
             nc.vector.tensor_tensor(window[cb][:].indirect(offsets[:]), own[cb][:], dif[cb][:], ADD)
             nc.sync.dma_start(out[block(cb), :], window[cb][:])

@@ -32,7 +32,7 @@ def tile_dgcn_b_kernel(tc, x, adj, w, b, base, offs, out):
     ):
         w_sb = held.tile([P, M, DB, C], BF16, name="w_sb")
         w_view = w.rearrange("m (db p) c -> p m db c", p=P)
-        nc.sync.dma_start(w_sb[:, M - 1 : M], w_view[:, M - 1 : M])
+        nc.scalar.dma_start(w_sb[:, M - 1 : M], w_view[:, M - 1 : M])
 
         x_sb = [held.tile([P, N], BF16, name=f"x_sb{db}") for db in range(DB)]
         for q in range(B):

@@ -9,6 +9,8 @@ S = 4096
 M = 4
 DB, CB, KB = D // P, C // P, NODES // P
 
+HALF = NODES // 2
+
 FLOPS = 2 * (3 * D * N * NODES + M * D * C * N)
 
 BF16, F32, U16 = mybir.dt.bfloat16, mybir.dt.float32, mybir.dt.uint16
@@ -159,14 +161,20 @@ def tile_dgcn_b_kernel(tc, x, adj, w, b, base, offs, out):
                     nc.tensor.transpose(plain_bank[:, block(kb)], twice_b2[cb][kb][:, block(q)], ident_bf16[:])
                 nc.scalar.copy(twice_b2_plain[cb][:, sample(q)], plain_bank[:])
 
-            for q in range(B):
-                dif_bank = banks.tile([P, NODES], F32, name="dif_bank", tag="bank")
+            for h in range(N // HALF):
+                columns = slice(h * HALF, (h + 1) * HALF)
+                nodes = slice(h % 2 * HALF, (h % 2 + 1) * HALF)
+                dif_bank = banks.tile([P, HALF], F32, name="dif_bank", tag="bank")
                 for kb in range(KB):
                     nc.tensor.matmul(
-                        dif_bank[:], b1[cb][kb][:, block(q)], sup_t[kb][:], start=(kb == 0), stop=(kb == KB - 1)
+                        dif_bank[:],
+                        b1[cb][kb][:, block(h // 2)],
+                        sup_t[kb][:, nodes],
+                        start=(kb == 0),
+                        stop=(kb == KB - 1),
                     )
                 nc.vector.scalar_tensor_tensor(
-                    dif[cb][:, sample(q)], twice_b2_plain[cb][:, sample(q)], -0.5, dif_bank[:], MULT, ADD
+                    dif[cb][:, columns], twice_b2_plain[cb][:, columns], -0.5, dif_bank[:], MULT, ADD
                 )
 
             nc.vector.tensor_tensor(window[cb][:].indirect(offsets[:]), own[cb][:], dif[cb][:], ADD)

@@ -10,6 +10,7 @@ M = 4
 DB, CB, KB = D // P, C // P, NODES // P
 
 HALF = NODES // 2
+assert B == KB
 
 FLOPS = 2 * (3 * D * N * NODES + M * D * C * N)
 
@@ -150,15 +151,16 @@ def tile_dgcn_b_kernel(tc, x, adj, w, b, base, offs, out):
 
             group = open_flipped(1, cb, closes=False)
             for nb in range(KB):
-                add_diffused(group[nb], nb, twice_b2[cb])
+                q = nb
+                plain_bank = banks.tile([P, NODES], BF16, name="plain_bank", tag="bank")
+                for kb in range(KB):
+                    nc.tensor.matmul(
+                        group[nb][:], sup_t[kb][:, block(nb)], twice_b2[cb][kb][:], start=False, stop=(kb == KB - 1)
+                    )
+                    nc.tensor.transpose(plain_bank[:, block(kb)], twice_b2[cb][kb][:, block(q)], ident_bf16[:])
                 nc.vector.scalar_tensor_tensor(
                     b1[cb][nb][:], twice_b3[cb][nb][:], -0.5, group[nb][:], MULT, ADD
                 )
-
-            for q in range(B):
-                plain_bank = banks.tile([P, NODES], BF16, name="plain_bank", tag="bank")
-                for kb in range(KB):
-                    nc.tensor.transpose(plain_bank[:, block(kb)], twice_b2[cb][kb][:, block(q)], ident_bf16[:])
                 nc.scalar.copy(twice_b2_plain[cb][:, sample(q)], plain_bank[:])
 
             for h in range(N // HALF):

@@ -120,10 +120,8 @@ def tile_dgcn_b_kernel(tc, x, adj, w, b, base, offs, out):
         row_sum = held.tile([P, KB], F32, name="row_sum")
         for kb in range(KB):
             nc.vector.reduce_sum(row_sum[:, kb : kb + 1], ah[kb][:], axis=mybir.AxisListType.X)
-        root = held.tile([P, KB], F32, name="root")
-        nc.scalar.activation(root[:], row_sum[:], ACT.Sqrt, bias=1.0)
         dis = held.tile([P, KB], F32, name="dis")
-        nc.vector.reciprocal(dis[:], root[:])
+        nc.scalar.activation(dis[:], row_sum[:], ACT.Abs_reciprocal_sqrt, bias=1.0)
 
         for kb in range(KB):
             nc.gpsimd.tensor_tensor(ah[kb][:, block(kb)], ah[kb][:, block(kb)], ident_f32[:], ADD)

import concourse.mybir as mybir
from concourse.masks import make_identity

P = 128
D, C = 256, 256
NODES, B = 512, 4
N = B * NODES
S = 4096
M = 4
DB, CB, KB = D // P, C // P, NODES // P

HALF = NODES // 2
assert B == KB

FLOPS = 2 * (3 * D * N * NODES + M * D * C * N)

BF16, F32, U16 = mybir.dt.bfloat16, mybir.dt.float32, mybir.dt.uint16
MULT, ADD = mybir.AluOpType.mult, mybir.AluOpType.add
ACT = mybir.ActivationFunctionType


def block(i):
    return slice(i * P, (i + 1) * P)


def sample(q):
    return slice(q * NODES, (q + 1) * NODES)


def tile_dgcn_b_kernel(tc, x, adj, w, b, base, offs, out):
    nc = tc.nc
    with (
        tc.tile_pool(name="held", bufs=1) as held,
        tc.psum_pool(name="banks", bufs=8) as banks,
    ):
        w_sb = held.tile([P, M, DB, C], BF16, name="w_sb")
        w_view = w.rearrange("m (db p) c -> p m db c", p=P)
        nc.scalar.dma_start(w_sb[:, M - 1 : M], w_view[:, M - 1 : M])

        x_sb = [held.tile([P, N], BF16, name=f"x_sb{db}") for db in range(DB)]
        for q in range(B):
            for db in range(DB):
                nc.sync.dma_start(x_sb[db][:, sample(q)], x[block(db), sample(q)])

        ah = [held.tile([P, NODES], F32, name=f"ah{kb}") for kb in range(KB)]
        for kb in range(KB):
            nc.scalar.dma_start(ah[kb][:], adj[block(kb), :])

        nc.sync.dma_start(w_sb[:, 0 : M - 1], w_view[:, 0 : M - 1])
        bias = [held.tile([P, 1], F32, name=f"bias{cb}") for cb in range(CB)]
        for cb in range(CB):
            nc.sync.dma_start(bias[cb][:], b[block(cb), :])

        offsets = held.tile([P, N // 16], U16, name="offsets")
        nc.sync.dma_start(offsets[:], offs)

        window = [held.tile([P, S], F32, name=f"window{cb}") for cb in range(CB)]
        for cb in range(CB):
            nc.sync.dma_start(window[cb][:], base[block(cb), :])

        ident_f32 = held.tile([P, P], F32, name="ident_f32")
        make_identity(nc, ident_f32[:])
        ident_bf16 = held.tile([P, P], BF16, name="ident_bf16")
        make_identity(nc, ident_bf16[:])

        def flipped_tiles(name):
            return [
                [held.tile([P, B * P], BF16, name=f"{name}_{cb}_{kb}") for kb in range(KB)] for cb in range(CB)
            ]

        twice_b3, twice_b2, b1 = flipped_tiles("twice_b3"), flipped_tiles("twice_b2"), flipped_tiles("b1")
        sup_t = [held.tile([P, NODES], BF16, name=f"sup_t{kb}") for kb in range(KB)]
        twice_b2_plain = [held.tile([P, N], BF16, name=f"twice_b2_plain{cb}") for cb in range(CB)]
        own = [held.tile([P, N], F32, name=f"own{cb}") for cb in range(CB)]
        dif = [held.tile([P, N], F32, name=f"dif{cb}") for cb in range(CB)]

        def open_flipped(m, cb, closes):
            group = [banks.tile([P, B * P], F32, name=f"flipped_bank{nb}", tag="bank") for nb in range(KB)]
            for q in range(B):
                for nb in range(KB):
                    for db in range(DB):
                        nc.tensor.matmul(
                            group[nb][:, block(q)],
                            x_sb[db][:, block(q * KB + nb)],
                            w_sb[:, m, db, block(cb)],
                            start=(q == 0 and db == 0),
                            stop=(closes and q == B - 1 and db == DB - 1),
                        )
            return group

        def add_diffused(bank, nb, source):
            for kb in range(KB):
                nc.tensor.matmul(
                    bank[:], sup_t[kb][:, block(nb)], source[kb][:], start=False, stop=(kb == KB - 1)
                )

        def start_recurrence(cb):
            group = open_flipped(3, cb, closes=True)
            for nb in range(KB):
                if nb % 2 == 0:
                    nc.scalar.activation(twice_b3[cb][nb][:], group[nb][:], ACT.Copy, scale=2.0)
                else:
                    nc.vector.tensor_scalar(twice_b3[cb][nb][:], group[nb][:], 2.0, None, MULT)

        def project_own(cb):
            for q in range(B):
                own_bank = banks.tile([P, NODES], F32, name="own_bank", tag="bank")
                for db in range(DB):
                    nc.tensor.matmul(
                        own_bank[:],
                        w_sb[:, 0, db, block(cb)],
                        x_sb[db][:, sample(q)],
                        start=(db == 0),
                        stop=(db == DB - 1),
                    )
                nc.scalar.activation(own[cb][:, sample(q)], own_bank[:], ACT.Identity, bias=bias[cb][:])

        start_recurrence(0)

        row_sum = held.tile([P, KB], F32, name="row_sum")
        for kb in range(KB):
            nc.vector.reduce_sum(row_sum[:, kb : kb + 1], ah[kb][:], axis=mybir.AxisListType.X)
        dis = held.tile([P, KB], F32, name="dis")
        nc.scalar.activation(dis[:], row_sum[:], ACT.Abs_reciprocal_sqrt, bias=1.0)

        for kb in range(KB):
            nc.gpsimd.tensor_tensor(ah[kb][:, block(kb)], ah[kb][:, block(kb)], ident_f32[:], ADD)

        dis_wide = held.tile([P, KB, P], F32, name="dis_wide")
        nc.vector.tensor_copy(dis_wide[:], dis[:].unsqueeze(2).to_broadcast([P, KB, P]))

        start_recurrence(1)
        project_own(0)

        dis_row = banks.tile([P, NODES], F32, name="dis_row", tag="bank")
        for kb in range(KB):
            nc.tensor.transpose(dis_row[:, block(kb)], dis_wide[:, kb, :], ident_f32[:])
        for kb in range(KB):
            nc.vector.scalar_tensor_tensor(sup_t[kb][:], ah[kb][:], dis[:, kb : kb + 1], dis_row[:], MULT, MULT)

        for cb in range(CB):
            if cb > 0:
                project_own(cb)

            group = open_flipped(2, cb, closes=False)
            for nb in range(KB):
                add_diffused(group[nb], nb, twice_b3[cb])
                nc.scalar.activation(twice_b2[cb][nb][:], group[nb][:], ACT.Copy, scale=2.0)

            group = open_flipped(1, cb, closes=False)
            for nb in range(KB):
                q = nb
                plain_bank = banks.tile([P, NODES], BF16, name="plain_bank", tag="bank")
                for kb in range(KB):
                    nc.tensor.matmul(
                        group[nb][:], sup_t[kb][:, block(nb)], twice_b2[cb][kb][:], start=False, stop=(kb == KB - 1)
                    )
                    nc.tensor.transpose(plain_bank[:, block(kb)], twice_b2[cb][kb][:, block(q)], ident_bf16[:])
                nc.vector.scalar_tensor_tensor(
                    b1[cb][nb][:], twice_b3[cb][nb][:], -0.5, group[nb][:], MULT, ADD
                )
                nc.scalar.copy(twice_b2_plain[cb][:, sample(q)], plain_bank[:])

            for h in range(N // HALF):
                columns = slice(h * HALF, (h + 1) * HALF)
                nodes = slice(h % 2 * HALF, (h % 2 + 1) * HALF)
                dif_bank = banks.tile([P, HALF], F32, name="dif_bank", tag="bank")
                for kb in range(KB):
                    nc.tensor.matmul(
                        dif_bank[:],
                        b1[cb][kb][:, block(h // 2)],
                        sup_t[kb][:, nodes],
                        start=(kb == 0),
                        stop=(kb == KB - 1),
                    )
                nc.vector.scalar_tensor_tensor(
                    dif[cb][:, columns], twice_b2_plain[cb][:, columns], -0.5, dif_bank[:], MULT, ADD
                )

            nc.vector.tensor_tensor(window[cb][:].indirect(offsets[:]), own[cb][:], dif[cb][:], ADD)
            nc.sync.dma_start(out[block(cb), :], window[cb][:])
